import numpy as np
import ml_dtypes


def mxq(x, axis, fmt="e4m3"):
    dtype, down = {"e4m3": (ml_dtypes.float8_e4m3fn, 7), "e5m2": (ml_dtypes.float8_e5m2, 14)}[fmt]
    v = np.moveaxis(np.asarray(x, np.float32).astype(ml_dtypes.bfloat16).astype(np.float64), axis, -1)
    blocks = v.reshape(v.shape[:-1] + (-1, 32))
    amax = np.abs(blocks).max(-1, keepdims=True)
    byte = np.maximum(np.where(amax > 0, np.frexp(amax)[1] - 1 + 127, 0) - down, 1)
    scale = np.exp2(byte - 127.0)
    codes = (blocks / scale).astype(np.float32).astype(dtype).astype(np.float64)
    return np.moveaxis((codes * scale).reshape(v.shape), -1, axis)


WIDE = False


def mx_kscale(k):
    if not WIDE:
        return np.ones(k)
    levels = np.array([10, -10, 5, -5, 0])
    a = np.random.permutation(np.resize(levels, k // 512 * 4)).reshape(k // 512, 4)
    idx = np.arange(k)
    return np.exp2(a[idx // 512, idx % 128 // 32])


BF16 = ml_dtypes.bfloat16


def bf(x):
    return np.asarray(x, np.float32).astype(BF16)


def f64(x):
    return np.asarray(x).astype(np.float64)


E2M1 = np.array([0.0, 0.5, 1.0, 1.5, 2.0, 3.0, 4.0, 6.0, -0.0, -0.5, -1.0, -1.5, -2.0, -3.0, -4.0, -6.0])


def pack_weight(w, fmt):
    k, n = w.shape
    w = f64(bf(w)).reshape(k // 32, 32, n)
    amax = np.abs(w).max(1)
    if fmt == "e4m3":
        byte = np.frexp(amax)[1] - 1 + 127 - 7
    else:
        mant, ex = np.frexp(amax / 6.0)
        byte = np.where(mant > 0.5, ex, ex - 1) + 127
    byte = np.clip(np.where(amax > 0, byte, 1), 1, 254)
    scaled = (w * np.exp2(127.0 - byte)[:, None, :]).reshape(k, n).astype(np.float32)
    by_word = np.ascontiguousarray(scaled.reshape(k // 512, 128, 4, n).transpose(0, 1, 3, 2))
    if fmt == "e4m3":
        words = by_word.astype(ml_dtypes.float8_e4m3fn).view(np.uint8)
    else:
        c = by_word.astype(ml_dtypes.float4_e2m1fn).view(np.uint8) & 0xF
        words = c[..., 0::2] | (c[..., 1::2] << 4)
    return np.ascontiguousarray(words), np.ascontiguousarray(byte.astype(np.uint8).reshape(k // 512, 16, n))


def unpack_weight(words, scales, fmt):
    g, p, n, _ = words.shape
    if fmt == "e4m3":
        vals = np.ascontiguousarray(words).view(ml_dtypes.float8_e4m3fn).astype(np.float64)
    else:
        nib = np.empty((g, p, n, 4), np.uint8)
        nib[..., 0::2] = words & 0xF
        nib[..., 1::2] = words >> 4
        vals = E2M1[nib]
    vals = vals * np.repeat(np.exp2(scales.astype(np.float64) - 127.0), 8, axis=1)[..., None]
    return vals.transpose(0, 1, 3, 2).reshape(g * 512, n)

def pack4(w):
    words, scales = pack_weight(w, "e2m1")
    return words.reshape(words.shape[0], 128, -1), scales


def unpack4(words, scales):
    return unpack_weight(words.reshape(words.shape[0], 128, -1, 2), scales, "e2m1")


B, C, H, W = 4, 512, 32, 32
GAMMA_INIT = 0.1


def setup_inputs():
    t = np.exp2(np.round(np.log2(mx_kscale(C)) / 2))
    gain = np.exp(0.5 * np.random.standard_normal((B, 1, H, W)))
    x = np.random.standard_normal((B, C, H, W)) * gain * t[None, :, None, None]
    gamma = (GAMMA_INIT * np.eye(C) + np.abs(np.random.standard_normal((C, C))) / C) / (t * t)[None, :]
    beta = 0.5 + np.random.random(C)
    gamma_words, gamma_scales = pack4(np.ascontiguousarray(gamma.T))
    return {"x": bf(x), "gamma_words": gamma_words, "gamma_scales": gamma_scales, "beta": bf(beta)}


def reference(x, gamma_words, gamma_scales, beta):
    xf = f64(x)
    sq = (xf * xf).reshape(B, C, H * W)
    norm = (unpack4(gamma_words, gamma_scales).T @ mxq(sq, 1, "e4m3")) + f64(beta)[None, :, None]
    return xf / np.sqrt(norm.reshape(B, C, H, W))

@@ -1,0 +1,109 @@
+from contextlib import ExitStack
+
+import concourse.mybir as mybir
+
+F32 = mybir.dt.float32
+BF16 = mybir.dt.bfloat16
+I32 = mybir.dt.int32
+U32 = mybir.dt.uint32
+U8 = mybir.dt.uint8
+FP8X4 = mybir.dt.float8_e4m3fn_x4
+FP4X4 = mybir.dt.float4_e2m1fn_x4
+ACT = mybir.ActivationFunctionType
+ALU = mybir.AluOpType
+
+P = 128
+B = 4
+C = 512
+HW = 1024
+PACK = 4
+MB = C // P
+NT = 512
+NH = HW // NT
+VW = 192
+
+FLOPS = 2 * C * C * B * HW
+
+
+def tile_gdn_kernel(tc, x, gamma_words, gamma_scales, beta, out):
+    nc = tc.nc
+    with ExitStack() as ctx:
+        const = ctx.enter_context(tc.tile_pool(name="const", bufs=1))
+        keep = ctx.enter_context(tc.tile_pool(name="keep", bufs=1))
+        work = ctx.enter_context(tc.tile_pool(name="work", bufs=3))
+        psum = ctx.enter_context(tc.psum_pool(name="psum", bufs=8))
+
+        w_words = const.tile([P, 2 * C], U8, align_bytes=64)
+        w_plane = const.tile([P, C], U8, align_bytes=64)
+        beta_bf = const.tile([P, MB], BF16)
+        beta_f = const.tile([P, MB], F32)
+        one = const.tile([P, 1], F32)
+        warm = const.tile([P, 1], F32)
+
+        nc.vector.memset(w_plane[:].bitcast(I32), 0)
+        nc.vector.memset(one[:], 1.0)
+        nc.scalar.activation(out=warm[:], in_=one[:], func=ACT.Abs_reciprocal_sqrt)
+
+        xa = [keep.tile([P, PACK, HW], BF16, name="xa%d" % b) for b in range(B)]
+        xb = [keep.tile([P, MB, HW], BF16, name="xb%d" % b) for b in range(B)]
+        res = [keep.tile([P, MB, HW], F32, name="res%d" % b) for b in range(B)]
+        xa_src = [x[b].rearrange("(p t) h w -> p t (h w)", t=PACK) for b in range(B)]
+        xb_src = [x[b].rearrange("(m r) h w -> r m (h w)", r=P) for b in range(B)]
+        out_dst = [out[b].rearrange("(m r) h w -> r m (h w)", r=P) for b in range(B)]
+
+        with nc.allow_non_contiguous_dma(reason="512 bias values, one to a partition and block"):
+            nc.scalar.dma_start(out=beta_bf[:], in_=beta.rearrange("(m r) -> r m", r=P))
+        for h in range(NH):
+            nc.sync.dma_start(out=xa[0][:, :, h * NT : (h + 1) * NT], in_=xa_src[0][:, :, h * NT : (h + 1) * NT])
+        nc.sync.dma_start(out=w_words[:].bitcast(I32), in_=gamma_words[0].bitcast(I32))
+        for q in range(4):
+            nc.sync.dma_start(
+                out=w_plane[32 * q : 32 * q + 4, :].bitcast(I32),
+                in_=gamma_scales[0, 4 * q : 4 * q + 4, :].bitcast(I32),
+            )
+        nc.sync.dma_start(out=xb[0][:], in_=xb_src[0])
+        for b in range(1, B):
+            nc.sync.dma_start(out=xa[b][:], in_=xa_src[b])
+            nc.sync.dma_start(out=xb[b][:], in_=xb_src[b])
+        nc.vector.tensor_copy(out=beta_f[:], in_=beta_bf[:])
+
+        for b in range(B):
+            codes = []
+            planes = []
+            for h in range(NH):
+                w0 = h * NT
+                grouped = work.tile([P, NT, PACK], BF16, align_bytes=64, name="grouped")
+                src_v = xa[b][:, :, w0 : w0 + VW].rearrange("p t w -> p w t")
+                src_s = xa[b][:, :, w0 + VW : w0 + NT].rearrange("p t w -> p w t")
+                nc.vector.tensor_tensor(out=grouped[:, 0:VW, :], in0=src_v, in1=src_v, op=ALU.mult)
+                nc.scalar.activation(out=grouped[:, VW:NT, :], in_=src_s, func=ACT.Square)
+                code = work.tile([P, NT], U32, align_bytes=64, name="code")
+                plane = work.tile([P, NT], U8, align_bytes=64, name="plane")
+                nc.vector.quantize_mx(
+                    out=code[:].bitcast(FP8X4),
+                    scales=plane[:],
+                    in_=grouped[:].rearrange("p w t -> p (w t)"),
+                )
+                codes.append(code)
+                planes.append(plane)
+            for m in range(MB):
+                for h in range(NH):
+                    acc = psum.tile([P, NT], F32, name="acc")
+                    nc.tensor.matmul_mx(
+                        out=acc[:],
+                        lhsT=w_words[:, 2 * P * m : 2 * P * (m + 1)].bitcast(FP4X4),
+                        lhsT_scale=w_plane[:, P * m : P * (m + 1)],
+                        rhs=codes[h][:].bitcast(FP8X4),
+                        rhs_scale=planes[h][:],
+                        start=True,
+                        stop=True,
+                    )
+                    nc.scalar.activation(
+                        out=res[b][:, m, h * NT : (h + 1) * NT],
+                        in_=acc[:],
+                        func=ACT.Abs_reciprocal_sqrt,
+                        bias=beta_f[:, m : m + 1],
+                        scale=1.0,
+                    )
+                nc.vector.tensor_tensor(out=res[b][:, m, :], in0=xb[b][:, m, :], in1=res[b][:, m, :], op=ALU.mult)
+                nc.sync.dma_start(out=out_dst[b][:, m, :], in_=res[b][:, m, :])

@@ -21,8 +21,21 @@ MB = C // P
 NT = 512
 NH = HW // NT
 VW = 192
+RUN_S = 1
+RUN_V = 1
+MANUAL = True
+TAIL_SPLIT = False
 
 FLOPS = 2 * C * C * B * HW
+
+
+def regroup_views(dst, src, run):
+    if run == 1:
+        return dst, src.rearrange("p t w -> p w t")
+    return (
+        dst.rearrange("p (c i) t -> p c t i", i=run),
+        src.rearrange("p t (c i) -> p c t i", i=run),
+    )
 
 
 def tile_gdn_kernel(tc, x, gamma_words, gamma_scales, beta, out):
@@ -30,80 +43,146 @@ def tile_gdn_kernel(tc, x, gamma_words, gamma_scales, beta, out):
     with ExitStack() as ctx:
         const = ctx.enter_context(tc.tile_pool(name="const", bufs=1))
         keep = ctx.enter_context(tc.tile_pool(name="keep", bufs=1))
-        work = ctx.enter_context(tc.tile_pool(name="work", bufs=3))
-        psum = ctx.enter_context(tc.psum_pool(name="psum", bufs=8))
+        psum = ctx.enter_context(tc.psum_pool(name="psum", bufs=1))
+        if MANUAL:
+            ctx.enter_context(tc.manual_schedule())
 
         w_words = const.tile([P, 2 * C], U8, align_bytes=64)
         w_plane = const.tile([P, C], U8, align_bytes=64)
         beta_bf = const.tile([P, MB], BF16)
-        beta_f = const.tile([P, MB], F32)
         one = const.tile([P, 1], F32)
         warm = const.tile([P, 1], F32)
+
+        xa = [keep.tile([P, PACK, HW], BF16, name="xa%d" % b) for b in range(B)]
+        xb = [keep.tile([P, MB, HW], BF16, name="xb%d" % b) for b in range(B)]
+        res = [keep.tile([P, MB, HW], F32, name="res%d" % b) for b in range(B)]
+        grouped = dict(
+            ((b, h), keep.tile([P, NT, PACK], BF16, align_bytes=64, name="grouped%d%d" % (b, h)))
+            for b in range(B)
+            for h in range(NH)
+        )
+        codes = dict(
+            ((b, h), keep.tile([P, NT], U32, align_bytes=64, name="codes%d%d" % (b, h)))
+            for b in range(B)
+            for h in range(NH)
+        )
+        planes = dict(
+            ((b, h), keep.tile([P, NT], U8, align_bytes=64, name="planes%d%d" % (b, h)))
+            for b in range(B)
+            for h in range(NH)
+        )
+        xa_src = [x[b].rearrange("(p t) h w -> p t (h w)", t=PACK) for b in range(B)]
+        xb_src = [x[b].rearrange("(m r) h w -> r m (h w)", r=P) for b in range(B)]
+        out_dst = [out[b].rearrange("(m r) h w -> r m (h w)", r=P) for b in range(B)]
+        acc = {}
 
         nc.vector.memset(w_plane[:].bitcast(I32), 0)
         nc.vector.memset(one[:], 1.0)
         nc.scalar.activation(out=warm[:], in_=one[:], func=ACT.Abs_reciprocal_sqrt)
 
-        xa = [keep.tile([P, PACK, HW], BF16, name="xa%d" % b) for b in range(B)]
-        xb = [keep.tile([P, MB, HW], BF16, name="xb%d" % b) for b in range(B)]
-        res = [keep.tile([P, MB, HW], F32, name="res%d" % b) for b in range(B)]
-        xa_src = [x[b].rearrange("(p t) h w -> p t (h w)", t=PACK) for b in range(B)]
-        xb_src = [x[b].rearrange("(m r) h w -> r m (h w)", r=P) for b in range(B)]
-        out_dst = [out[b].rearrange("(m r) h w -> r m (h w)", r=P) for b in range(B)]
-
-        with nc.allow_non_contiguous_dma(reason="512 bias values, one to a partition and block"):
-            nc.scalar.dma_start(out=beta_bf[:], in_=beta.rearrange("(m r) -> r m", r=P))
-        for h in range(NH):
-            nc.sync.dma_start(out=xa[0][:, :, h * NT : (h + 1) * NT], in_=xa_src[0][:, :, h * NT : (h + 1) * NT])
+        nc.sync.dma_start(out=xa[0][:, :, 0:NT], in_=xa_src[0][:, :, 0:NT])
         nc.sync.dma_start(out=w_words[:].bitcast(I32), in_=gamma_words[0].bitcast(I32))
         for q in range(4):
             nc.sync.dma_start(
                 out=w_plane[32 * q : 32 * q + 4, :].bitcast(I32),
                 in_=gamma_scales[0, 4 * q : 4 * q + 4, :].bitcast(I32),
             )
+        nc.sync.dma_start(out=xa[0][:, :, NT:HW], in_=xa_src[0][:, :, NT:HW])
+        nc.sync.dma_start(out=xa[1][:], in_=xa_src[1])
+        with nc.allow_non_contiguous_dma(reason="512 bias values, one to a partition and block"):
+            nc.sync.dma_start(out=beta_bf[:], in_=beta.rearrange("(m r) -> r m", r=P))
         nc.sync.dma_start(out=xb[0][:], in_=xb_src[0])
-        for b in range(1, B):
+        for b in range(2, B):
             nc.sync.dma_start(out=xa[b][:], in_=xa_src[b])
-            nc.sync.dma_start(out=xb[b][:], in_=xb_src[b])
-        nc.vector.tensor_copy(out=beta_f[:], in_=beta_bf[:])
+            nc.sync.dma_start(out=xb[b - 1][:], in_=xb_src[b - 1])
+        nc.sync.dma_start(out=xb[B - 1][:], in_=xb_src[B - 1])
 
-        for b in range(B):
-            codes = []
-            planes = []
+        def sq_v(b, h):
+            w0 = h * NT
+            dst, src = regroup_views(grouped[(b, h)][:, 0:VW, :], xa[b][:, :, w0 : w0 + VW], RUN_V)
+            nc.vector.tensor_tensor(out=dst, in0=src, in1=src, op=ALU.mult)
+
+        def sq_s(b, h):
+            w0 = h * NT
+            dst, src = regroup_views(grouped[(b, h)][:, VW:NT, :], xa[b][:, :, w0 + VW : w0 + NT], RUN_S)
+            nc.scalar.activation(out=dst, in_=src, func=ACT.Square)
+
+        def quant(b, h):
+            nc.vector.quantize_mx(
+                out=codes[(b, h)][:].bitcast(FP8X4),
+                scales=planes[(b, h)][:],
+                in_=grouped[(b, h)][:].rearrange("p w t -> p (w t)"),
+            )
+
+        def mx(b, m, h):
+            acc[(b, m, h)] = psum.tile([P, NT], F32, name="acc%d%d" % (m, h))
+            nc.tensor.matmul_mx(
+                out=acc[(b, m, h)][:],
+                lhsT=w_words[:, 2 * P * m : 2 * P * (m + 1)].bitcast(FP4X4),
+                lhsT_scale=w_plane[:, P * m : P * (m + 1)],
+                rhs=codes[(b, h)][:].bitcast(FP8X4),
+                rhs_scale=planes[(b, h)][:],
+                start=True,
+                stop=True,
+            )
+
+        def rs(b, m, h):
+            nc.scalar.activation(
+                out=res[b][:, m, h * NT : (h + 1) * NT],
+                in_=acc[(b, m, h)][:],
+                func=ACT.Abs_reciprocal_sqrt,
+                bias=beta_bf[:, m : m + 1],
+                scale=1.0,
+            )
+
+        def mul_store(b, m, lo, hi):
+            nc.vector.tensor_tensor(
+                out=res[b][:, m, lo:hi], in0=xb[b][:, m, lo:hi], in1=res[b][:, m, lo:hi], op=ALU.mult
+            )
+            nc.sync.dma_start(out=out_dst[b][:, m, lo:hi], in_=res[b][:, m, lo:hi])
+
+        sq_v(0, 0)
+        sq_s(0, 0)
+        quant(0, 0)
+        sq_v(0, 1)
+        sq_s(0, 1)
+        quant(0, 1)
+        for m in range(MB):
             for h in range(NH):
-                w0 = h * NT
-                grouped = work.tile([P, NT, PACK], BF16, align_bytes=64, name="grouped")
-                src_v = xa[b][:, :, w0 : w0 + VW].rearrange("p t w -> p w t")
-                src_s = xa[b][:, :, w0 + VW : w0 + NT].rearrange("p t w -> p w t")
-                nc.vector.tensor_tensor(out=grouped[:, 0:VW, :], in0=src_v, in1=src_v, op=ALU.mult)
-                nc.scalar.activation(out=grouped[:, VW:NT, :], in_=src_s, func=ACT.Square)
-                code = work.tile([P, NT], U32, align_bytes=64, name="code")
-                plane = work.tile([P, NT], U8, align_bytes=64, name="plane")
-                nc.vector.quantize_mx(
-                    out=code[:].bitcast(FP8X4),
-                    scales=plane[:],
-                    in_=grouped[:].rearrange("p w t -> p (w t)"),
-                )
-                codes.append(code)
-                planes.append(plane)
-            for m in range(MB):
-                for h in range(NH):
-                    acc = psum.tile([P, NT], F32, name="acc")
-                    nc.tensor.matmul_mx(
-                        out=acc[:],
-                        lhsT=w_words[:, 2 * P * m : 2 * P * (m + 1)].bitcast(FP4X4),
-                        lhsT_scale=w_plane[:, P * m : P * (m + 1)],
-                        rhs=codes[h][:].bitcast(FP8X4),
-                        rhs_scale=planes[h][:],
-                        start=True,
-                        stop=True,
-                    )
-                    nc.scalar.activation(
-                        out=res[b][:, m, h * NT : (h + 1) * NT],
-                        in_=acc[:],
-                        func=ACT.Abs_reciprocal_sqrt,
-                        bias=beta_f[:, m : m + 1],
-                        scale=1.0,
-                    )
-                nc.vector.tensor_tensor(out=res[b][:, m, :], in0=xb[b][:, m, :], in1=res[b][:, m, :], op=ALU.mult)
-                nc.sync.dma_start(out=out_dst[b][:, m, :], in_=res[b][:, m, :])
+                mx(0, m, h)
+
+        for a in range(B):
+            b = a + 1
+            more = b < B
+            if more:
+                sq_v(b, 0)
+            rs(a, 0, 0)
+            if more:
+                sq_s(b, 0)
+                quant(b, 0)
+            rs(a, 0, 1)
+            mul_store(a, 0, 0, HW)
+            if more:
+                sq_v(b, 1)
+            rs(a, 1, 0)
+            rs(a, 1, 1)
+            mul_store(a, 1, 0, HW)
+            if more:
+                sq_s(b, 1)
+                quant(b, 1)
+                for m in range(2):
+                    for h in range(NH):
+                        mx(b, m, h)
+            for m in range(2, MB):
+                last = TAIL_SPLIT and (not more) and m == MB - 1
+                rs(a, m, 0)
+                if last:
+                    mul_store(a, m, 0, NT)
+                rs(a, m, 1)
+                if more:
+                    mx(b, m, 0)
+                    mx(b, m, 1)
+                if last:
+                    mul_store(a, m, NT, HW)
+                else:
+                    mul_store(a, m, 0, HW)

@@ -21,10 +21,10 @@ MB = C // P
 NT = 512
 NH = HW // NT
 VW = 192
-RUN_S = 1
-RUN_V = 1
+RUN_S = 4
+RUN_V = 4
 MANUAL = True
-TAIL_SPLIT = False
+TAIL_SPLIT = True
 
 FLOPS = 2 * C * C * B * HW
 

@@ -1,6 +1,7 @@
 from contextlib import ExitStack
 
 import concourse.mybir as mybir
+from concourse.masks import make_identity
 
 F32 = mybir.dt.float32
 BF16 = mybir.dt.bfloat16
@@ -20,11 +21,10 @@ PACK = 4
 MB = C // P
 NT = 512
 NH = HW // NT
-VW = 192
-RUN_S = 4
-RUN_V = 4
-MANUAL = True
-TAIL_SPLIT = True
+KW = HW // 2 // P
+KH = KW // NH
+VW = 160
+RUN = 4
 
 FLOPS = 2 * C * C * B * HW
 
@@ -44,17 +44,25 @@ def tile_gdn_kernel(tc, x, gamma_words, gamma_scales, beta, out):
         const = ctx.enter_context(tc.tile_pool(name="const", bufs=1))
         keep = ctx.enter_context(tc.tile_pool(name="keep", bufs=1))
         psum = ctx.enter_context(tc.psum_pool(name="psum", bufs=1))
-        if MANUAL:
-            ctx.enter_context(tc.manual_schedule())
+        ctx.enter_context(tc.manual_schedule())
 
         w_words = const.tile([P, 2 * C], U8, align_bytes=64)
         w_plane = const.tile([P, C], U8, align_bytes=64)
         beta_bf = const.tile([P, MB], BF16)
         one = const.tile([P, 1], F32)
         warm = const.tile([P, 1], F32)
+        ident = const.tile([P, P], F32)
 
-        xa = [keep.tile([P, PACK, HW], BF16, name="xa%d" % b) for b in range(B)]
-        xb = [keep.tile([P, MB, HW], BF16, name="xb%d" % b) for b in range(B)]
+        xa = dict(
+            ((b, h), keep.tile([P, PACK, NT], BF16, name="xa%d%d" % (b, h))) for b in range(1) for h in range(NH)
+        )
+        for b in range(1, B):
+            whole = keep.tile([P, PACK, HW], BF16, name="xa%d" % b)
+            for h in range(NH):
+                xa[(b, h)] = whole[:, :, h * NT : (h + 1) * NT]
+            xa[b] = whole
+        xb = dict((b, keep.tile([P, MB, HW], BF16, name="xb%d" % b)) for b in range(1, B))
+        yy = keep.tile([P, KW, C], F32, name="yy")
         res = [keep.tile([P, MB, HW], F32, name="res%d" % b) for b in range(B)]
         grouped = dict(
             ((b, h), keep.tile([P, NT, PACK], BF16, align_bytes=64, name="grouped%d%d" % (b, h)))
@@ -75,36 +83,41 @@ def tile_gdn_kernel(tc, x, gamma_words, gamma_scales, beta, out):
         xb_src = [x[b].rearrange("(m r) h w -> r m (h w)", r=P) for b in range(B)]
         out_dst = [out[b].rearrange("(m r) h w -> r m (h w)", r=P) for b in range(B)]
         acc = {}
+        t1 = {}
+        t2 = {}
 
         nc.vector.memset(w_plane[:].bitcast(I32), 0)
         nc.vector.memset(one[:], 1.0)
         nc.scalar.activation(out=warm[:], in_=one[:], func=ACT.Abs_reciprocal_sqrt)
+        make_identity(nc, ident[:])
 
-        nc.sync.dma_start(out=xa[0][:, :, 0:NT], in_=xa_src[0][:, :, 0:NT])
+        nc.sync.dma_start(out=xa[(0, 0)][:], in_=xa_src[0][:, :, 0:NT])
         nc.sync.dma_start(out=w_words[:].bitcast(I32), in_=gamma_words[0].bitcast(I32))
         for q in range(4):
             nc.sync.dma_start(
                 out=w_plane[32 * q : 32 * q + 4, :].bitcast(I32),
                 in_=gamma_scales[0, 4 * q : 4 * q + 4, :].bitcast(I32),
             )
-        nc.sync.dma_start(out=xa[0][:, :, NT:HW], in_=xa_src[0][:, :, NT:HW])
+        nc.sync.dma_start(out=xa[(0, 1)][:], in_=xa_src[0][:, :, NT:HW])
         nc.sync.dma_start(out=xa[1][:], in_=xa_src[1])
         with nc.allow_non_contiguous_dma(reason="512 bias values, one to a partition and block"):
             nc.sync.dma_start(out=beta_bf[:], in_=beta.rearrange("(m r) -> r m", r=P))
-        nc.sync.dma_start(out=xb[0][:], in_=xb_src[0])
         for b in range(2, B):
             nc.sync.dma_start(out=xa[b][:], in_=xa_src[b])
             nc.sync.dma_start(out=xb[b - 1][:], in_=xb_src[b - 1])
         nc.sync.dma_start(out=xb[B - 1][:], in_=xb_src[B - 1])
 
+        def half(b, h):
+            if b == 0:
+                return xa[(b, h)][:]
+            return xa[(b, h)]
+
         def sq_v(b, h):
-            w0 = h * NT
-            dst, src = regroup_views(grouped[(b, h)][:, 0:VW, :], xa[b][:, :, w0 : w0 + VW], RUN_V)
+            dst, src = regroup_views(grouped[(b, h)][:, 0:VW, :], half(b, h)[:, :, 0:VW], RUN)
             nc.vector.tensor_tensor(out=dst, in0=src, in1=src, op=ALU.mult)
 
         def sq_s(b, h):
-            w0 = h * NT
-            dst, src = regroup_views(grouped[(b, h)][:, VW:NT, :], xa[b][:, :, w0 + VW : w0 + NT], RUN_S)
+            dst, src = regroup_views(grouped[(b, h)][:, VW:NT, :], half(b, h)[:, :, VW:NT], RUN)
             nc.scalar.activation(out=dst, in_=src, func=ACT.Square)
 
         def quant(b, h):
@@ -115,7 +128,7 @@ def tile_gdn_kernel(tc, x, gamma_words, gamma_scales, beta, out):
             )
 
         def mx(b, m, h):
-            acc[(b, m, h)] = psum.tile([P, NT], F32, name="acc%d%d" % (m, h))
+            acc[(b, m, h)] = psum.tile([P, NT], F32, name="bank%d" % (2 * (m % 2) + h))
             nc.tensor.matmul_mx(
                 out=acc[(b, m, h)][:],
                 lhsT=w_words[:, 2 * P * m : 2 * P * (m + 1)].bitcast(FP4X4),
@@ -135,21 +148,50 @@ def tile_gdn_kernel(tc, x, gamma_words, gamma_scales, beta, out):
                 scale=1.0,
             )
 
-        def mul_store(b, m, lo, hi):
-            nc.vector.tensor_tensor(
-                out=res[b][:, m, lo:hi], in0=xb[b][:, m, lo:hi], in1=res[b][:, m, lo:hi], op=ALU.mult
+        def turn1(k):
+            t1[k] = psum.tile([P, PACK, P], F32, name="bank%d" % (4 + k))
+            words = xa[(0, k // KH)][:].bitcast(F32)
+            for t in range(PACK):
+                nc.tensor.transpose(t1[k][:, t, :], words[:, t, P * (k % KH) : P * (k % KH + 1)], ident[:])
+
+        def evac(k):
+            nc.vector.tensor_copy(
+                out=yy[:, k, :].rearrange("q (p t) -> q p t", t=PACK), in_=t1[k][:].rearrange("q t p -> q p t")
             )
+
+        def turn2(m):
+            t2[m] = psum.tile([P, KW, P], F32, name="bank%d" % (4 + m))
+            for k in range(KW):
+                nc.tensor.transpose(t2[m][:, k, :], yy[:, k, P * m : P * (m + 1)], ident[:])
+
+        def mul_store(b, m, lo, hi):
+            if b == 0:
+                num = t2[m][:].rearrange("r k q -> r (k q)").bitcast(BF16)[:, lo:hi]
+            else:
+                num = xb[b][:, m, lo:hi]
+            nc.vector.tensor_tensor(out=res[b][:, m, lo:hi], in0=num, in1=res[b][:, m, lo:hi], op=ALU.mult)
             nc.sync.dma_start(out=out_dst[b][:, m, lo:hi], in_=res[b][:, m, lo:hi])
 
+        turn1(0)
+        turn1(1)
+        turn1(2)
         sq_v(0, 0)
         sq_s(0, 0)
+        evac(0)
         quant(0, 0)
+        mx(0, 0, 0)
+        mx(0, 1, 0)
+        turn1(3)
+        evac(1)
         sq_v(0, 1)
         sq_s(0, 1)
         quant(0, 1)
+        mx(0, 0, 1)
+        mx(0, 1, 1)
+        evac(2)
+        evac(3)
         for m in range(MB):
-            for h in range(NH):
-                mx(0, m, h)
+            turn2(m)
 
         for a in range(B):
             b = a + 1
@@ -161,28 +203,32 @@ def tile_gdn_kernel(tc, x, gamma_words, gamma_scales, beta, out):
                 sq_s(b, 0)
                 quant(b, 0)
             rs(a, 0, 1)
+            mx(a, 2, 0)
+            mx(a, 2, 1)
             mul_store(a, 0, 0, HW)
             if more:
                 sq_v(b, 1)
             rs(a, 1, 0)
             rs(a, 1, 1)
+            mx(a, 3, 0)
+            mx(a, 3, 1)
             mul_store(a, 1, 0, HW)
             if more:
                 sq_s(b, 1)
                 quant(b, 1)
-                for m in range(2):
-                    for h in range(NH):
-                        mx(b, m, h)
-            for m in range(2, MB):
-                last = TAIL_SPLIT and (not more) and m == MB - 1
-                rs(a, m, 0)
-                if last:
-                    mul_store(a, m, 0, NT)
-                rs(a, m, 1)
-                if more:
-                    mx(b, m, 0)
-                    mx(b, m, 1)
-                if last:
-                    mul_store(a, m, NT, HW)
-                else:
-                    mul_store(a, m, 0, HW)
+            rs(a, 2, 0)
+            rs(a, 2, 1)
+            if more:
+                mx(b, 0, 0)
+                mx(b, 0, 1)
+            mul_store(a, 2, 0, HW)
+            rs(a, 3, 0)
+            if not more:
+                mul_store(a, 3, 0, NT)
+            rs(a, 3, 1)
+            if more:
+                mx(b, 1, 0)
+                mx(b, 1, 1)
+                mul_store(a, 3, 0, HW)
+            else:
+                mul_store(a, 3, NT, HW)

@@ -1,7 +1,6 @@
 from contextlib import ExitStack
 
 import concourse.mybir as mybir
-from concourse.masks import make_identity
 
 F32 = mybir.dt.float32
 BF16 = mybir.dt.bfloat16
@@ -18,20 +17,16 @@ B = 4
 C = 512
 HW = 1024
 PACK = 4
-MB = C // P
 NT = 512
 NH = HW // NT
-KW = HW // 2 // P
-KH = KW // NH
-VW = 160
+UNITS = B * NH
+VW = 192
 RUN = 4
 
 FLOPS = 2 * C * C * B * HW
 
 
 def regroup_views(dst, src, run):
-    if run == 1:
-        return dst, src.rearrange("p t w -> p w t")
     return (
         dst.rearrange("p (c i) t -> p c t i", i=run),
         src.rearrange("p t (c i) -> p c t i", i=run),
@@ -46,189 +41,121 @@ def tile_gdn_kernel(tc, x, gamma_words, gamma_scales, beta, out):
         psum = ctx.enter_context(tc.psum_pool(name="psum", bufs=1))
         ctx.enter_context(tc.manual_schedule())
 
+        w_raw = const.tile([P, 2 * C], U8, align_bytes=64)
         w_words = const.tile([P, 2 * C], U8, align_bytes=64)
+        s_raw = const.tile([P, C], U8, align_bytes=64)
         w_plane = const.tile([P, C], U8, align_bytes=64)
-        beta_bf = const.tile([P, MB], BF16)
+        beta_bf = const.tile([P, PACK], BF16)
         one = const.tile([P, 1], F32)
         warm = const.tile([P, 1], F32)
-        ident = const.tile([P, P], F32)
 
-        xa = dict(
-            ((b, h), keep.tile([P, PACK, NT], BF16, name="xa%d%d" % (b, h))) for b in range(1) for h in range(NH)
-        )
+        xs = {}
+        for h in range(NH):
+            first = keep.tile([P, PACK, NT], BF16, name="xa0%d" % h)
+            xs[h] = first[:]
+        whole = {}
         for b in range(1, B):
-            whole = keep.tile([P, PACK, HW], BF16, name="xa%d" % b)
+            whole[b] = keep.tile([P, PACK, HW], BF16, name="xa%d" % b)
             for h in range(NH):
-                xa[(b, h)] = whole[:, :, h * NT : (h + 1) * NT]
-            xa[b] = whole
-        xb = dict((b, keep.tile([P, MB, HW], BF16, name="xb%d" % b)) for b in range(1, B))
-        yy = keep.tile([P, KW, C], F32, name="yy")
-        res = [keep.tile([P, MB, HW], F32, name="res%d" % b) for b in range(B)]
-        grouped = dict(
-            ((b, h), keep.tile([P, NT, PACK], BF16, align_bytes=64, name="grouped%d%d" % (b, h)))
-            for b in range(B)
-            for h in range(NH)
-        )
-        codes = dict(
-            ((b, h), keep.tile([P, NT], U32, align_bytes=64, name="codes%d%d" % (b, h)))
-            for b in range(B)
-            for h in range(NH)
-        )
-        planes = dict(
-            ((b, h), keep.tile([P, NT], U8, align_bytes=64, name="planes%d%d" % (b, h)))
-            for b in range(B)
-            for h in range(NH)
-        )
-        xa_src = [x[b].rearrange("(p t) h w -> p t (h w)", t=PACK) for b in range(B)]
-        xb_src = [x[b].rearrange("(m r) h w -> r m (h w)", r=P) for b in range(B)]
-        out_dst = [out[b].rearrange("(m r) h w -> r m (h w)", r=P) for b in range(B)]
+                xs[NH * b + h] = whole[b][:, :, h * NT : (h + 1) * NT]
+        res = [keep.tile([P, PACK, NT], F32, name="res%d" % u) for u in range(UNITS)]
+        grouped = [keep.tile([P, NT, PACK], BF16, align_bytes=64, name="grouped%d" % u) for u in range(UNITS)]
+        codes = [keep.tile([P, NT], U32, align_bytes=64, name="codes%d" % u) for u in range(UNITS)]
+        planes = [keep.tile([P, NT], U8, align_bytes=64, name="planes%d" % u) for u in range(UNITS)]
+        x_src = [x[b].rearrange("(p t) h w -> p t (h w)", t=PACK) for b in range(B)]
+        out_dst = [out[b].rearrange("(p t) h w -> p t (h w)", t=PACK) for b in range(B)]
         acc = {}
-        t1 = {}
-        t2 = {}
 
-        nc.vector.memset(w_plane[:].bitcast(I32), 0)
+        nc.vector.memset(s_raw[:].bitcast(I32), 0)
         nc.vector.memset(one[:], 1.0)
         nc.scalar.activation(out=warm[:], in_=one[:], func=ACT.Abs_reciprocal_sqrt)
-        make_identity(nc, ident[:])
 
-        nc.sync.dma_start(out=xa[(0, 0)][:], in_=xa_src[0][:, :, 0:NT])
-        nc.sync.dma_start(out=w_words[:].bitcast(I32), in_=gamma_words[0].bitcast(I32))
+        nc.sync.dma_start(out=xs[0], in_=x_src[0][:, :, 0:NT])
+        nc.sync.dma_start(out=w_raw[:].bitcast(I32), in_=gamma_words[0].bitcast(I32))
         for q in range(4):
             nc.sync.dma_start(
-                out=w_plane[32 * q : 32 * q + 4, :].bitcast(I32),
+                out=s_raw[32 * q : 32 * q + 4, :].bitcast(I32),
                 in_=gamma_scales[0, 4 * q : 4 * q + 4, :].bitcast(I32),
             )
-        nc.sync.dma_start(out=xa[(0, 1)][:], in_=xa_src[0][:, :, NT:HW])
-        nc.sync.dma_start(out=xa[1][:], in_=xa_src[1])
-        with nc.allow_non_contiguous_dma(reason="512 bias values, one to a partition and block"):
-            nc.sync.dma_start(out=beta_bf[:], in_=beta.rearrange("(m r) -> r m", r=P))
-        for b in range(2, B):
-            nc.sync.dma_start(out=xa[b][:], in_=xa_src[b])
-            nc.sync.dma_start(out=xb[b - 1][:], in_=xb_src[b - 1])
-        nc.sync.dma_start(out=xb[B - 1][:], in_=xb_src[B - 1])
+        nc.sync.dma_start(out=xs[1], in_=x_src[0][:, :, NT:HW])
+        nc.sync.dma_start(out=beta_bf[:], in_=beta.rearrange("(p t) -> p t", t=PACK))
+        for b in range(1, B):
+            nc.sync.dma_start(out=whole[b][:], in_=x_src[b])
 
-        def half(b, h):
-            if b == 0:
-                return xa[(b, h)][:]
-            return xa[(b, h)]
-
-        def sq_v(b, h):
-            dst, src = regroup_views(grouped[(b, h)][:, 0:VW, :], half(b, h)[:, :, 0:VW], RUN)
+        def sq_v(u):
+            dst, src = regroup_views(grouped[u][:, 0:VW, :], xs[u][:, :, 0:VW], RUN)
             nc.vector.tensor_tensor(out=dst, in0=src, in1=src, op=ALU.mult)
 
-        def sq_s(b, h):
-            dst, src = regroup_views(grouped[(b, h)][:, VW:NT, :], half(b, h)[:, :, VW:NT], RUN)
+        def sq_s(u):
+            dst, src = regroup_views(grouped[u][:, VW:NT, :], xs[u][:, :, VW:NT], RUN)
             nc.scalar.activation(out=dst, in_=src, func=ACT.Square)
 
-        def quant(b, h):
+        def quant(u):
             nc.vector.quantize_mx(
-                out=codes[(b, h)][:].bitcast(FP8X4),
-                scales=planes[(b, h)][:],
-                in_=grouped[(b, h)][:].rearrange("p w t -> p (w t)"),
+                out=codes[u][:].bitcast(FP8X4),
+                scales=planes[u][:],
+                in_=grouped[u][:].rearrange("p w t -> p (w t)"),
             )
 
-        def mx(b, m, h):
-            acc[(b, m, h)] = psum.tile([P, NT], F32, name="bank%d" % (2 * (m % 2) + h))
+        def mx(u, t):
+            acc[(u, t)] = psum.tile([P, NT], F32, name="bank%d" % (PACK * (u % 2) + t))
             nc.tensor.matmul_mx(
-                out=acc[(b, m, h)][:],
-                lhsT=w_words[:, 2 * P * m : 2 * P * (m + 1)].bitcast(FP4X4),
-                lhsT_scale=w_plane[:, P * m : P * (m + 1)],
-                rhs=codes[(b, h)][:].bitcast(FP8X4),
-                rhs_scale=planes[(b, h)][:],
+                out=acc[(u, t)][:],
+                lhsT=w_words[:, 2 * P * t : 2 * P * (t + 1)].bitcast(FP4X4),
+                lhsT_scale=w_plane[:, P * t : P * (t + 1)],
+                rhs=codes[u][:].bitcast(FP8X4),
+                rhs_scale=planes[u][:],
                 start=True,
                 stop=True,
             )
 
-        def rs(b, m, h):
+        def rs(u, t):
             nc.scalar.activation(
-                out=res[b][:, m, h * NT : (h + 1) * NT],
-                in_=acc[(b, m, h)][:],
+                out=res[u][:, t, :],
+                in_=acc[(u, t)][:],
                 func=ACT.Abs_reciprocal_sqrt,
-                bias=beta_bf[:, m : m + 1],
+                bias=beta_bf[:, t : t + 1],
                 scale=1.0,
             )
 
-        def turn1(k):
-            t1[k] = psum.tile([P, PACK, P], F32, name="bank%d" % (4 + k))
-            words = xa[(0, k // KH)][:].bitcast(F32)
-            for t in range(PACK):
-                nc.tensor.transpose(t1[k][:, t, :], words[:, t, P * (k % KH) : P * (k % KH + 1)], ident[:])
-
-        def evac(k):
-            nc.vector.tensor_copy(
-                out=yy[:, k, :].rearrange("q (p t) -> q p t", t=PACK), in_=t1[k][:].rearrange("q t p -> q p t")
+        def mul_store(u, t0, t1):
+            nc.vector.tensor_tensor(
+                out=res[u][:, t0:t1, :], in0=xs[u][:, t0:t1, :], in1=res[u][:, t0:t1, :], op=ALU.mult
             )
+            h = u % NH
+            nc.sync.dma_start(out=out_dst[u // NH][:, t0:t1, h * NT : (h + 1) * NT], in_=res[u][:, t0:t1, :])
 
-        def turn2(m):
-            t2[m] = psum.tile([P, KW, P], F32, name="bank%d" % (4 + m))
-            for k in range(KW):
-                nc.tensor.transpose(t2[m][:, k, :], yy[:, k, P * m : P * (m + 1)], ident[:])
+        sq_v(0)
+        sq_s(0)
+        nc.vector.tensor_copy(
+            out=w_words[:].rearrange("p (t q e) -> p q t e", t=PACK, e=2),
+            in_=w_raw[:].rearrange("p (q t e) -> p q t e", t=PACK, e=2),
+        )
+        nc.vector.tensor_copy(
+            out=w_plane[:].rearrange("p (t q) -> p q t", t=PACK),
+            in_=s_raw[:].rearrange("p (q t) -> p q t", t=PACK),
+        )
+        quant(0)
+        for t in range(PACK):
+            mx(0, t)
 
-        def mul_store(b, m, lo, hi):
-            if b == 0:
-                num = t2[m][:].rearrange("r k q -> r (k q)").bitcast(BF16)[:, lo:hi]
-            else:
-                num = xb[b][:, m, lo:hi]
-            nc.vector.tensor_tensor(out=res[b][:, m, lo:hi], in0=num, in1=res[b][:, m, lo:hi], op=ALU.mult)
-            nc.sync.dma_start(out=out_dst[b][:, m, lo:hi], in_=res[b][:, m, lo:hi])
-
-        turn1(0)
-        turn1(1)
-        turn1(2)
-        sq_v(0, 0)
-        sq_s(0, 0)
-        evac(0)
-        quant(0, 0)
-        mx(0, 0, 0)
-        mx(0, 1, 0)
-        turn1(3)
-        evac(1)
-        sq_v(0, 1)
-        sq_s(0, 1)
-        quant(0, 1)
-        mx(0, 0, 1)
-        mx(0, 1, 1)
-        evac(2)
-        evac(3)
-        for m in range(MB):
-            turn2(m)
-
-        for a in range(B):
-            b = a + 1
-            more = b < B
+        for u in range(UNITS):
+            n = u + 1
+            more = n < UNITS
             if more:
-                sq_v(b, 0)
-            rs(a, 0, 0)
+                sq_v(n)
+                sq_s(n)
+            rs(u, 0)
+            if u > 0:
+                mul_store(u - 1, 2, 4)
             if more:
-                sq_s(b, 0)
-                quant(b, 0)
-            rs(a, 0, 1)
-            mx(a, 2, 0)
-            mx(a, 2, 1)
-            mul_store(a, 0, 0, HW)
+                quant(n)
+            rs(u, 1)
             if more:
-                sq_v(b, 1)
-            rs(a, 1, 0)
-            rs(a, 1, 1)
-            mx(a, 3, 0)
-            mx(a, 3, 1)
-            mul_store(a, 1, 0, HW)
-            if more:
-                sq_s(b, 1)
-                quant(b, 1)
-            rs(a, 2, 0)
-            rs(a, 2, 1)
-            if more:
-                mx(b, 0, 0)
-                mx(b, 0, 1)
-            mul_store(a, 2, 0, HW)
-            rs(a, 3, 0)
-            if not more:
-                mul_store(a, 3, 0, NT)
-            rs(a, 3, 1)
-            if more:
-                mx(b, 1, 0)
-                mx(b, 1, 1)
-                mul_store(a, 3, 0, HW)
-            else:
-                mul_store(a, 3, NT, HW)
+                for t in range(PACK):
+                    mx(n, t)
+            mul_store(u, 0, 2)
+            rs(u, 2)
+            rs(u, 3)
+        mul_store(UNITS - 1, 2, 3)
+        mul_store(UNITS - 1, 3, 4)

@@ -20,8 +20,10 @@ PACK = 4
 NT = 512
 NH = HW // NT
 UNITS = B * NH
-VW = 192
+VNUM = 3
+VDEN = 8
 RUN = 4
+AHEAD = 3
 
 FLOPS = 2 * C * C * B * HW
 
@@ -49,46 +51,59 @@ def tile_gdn_kernel(tc, x, gamma_words, gamma_scales, beta, out):
         one = const.tile([P, 1], F32)
         warm = const.tile([P, 1], F32)
 
-        xs = {}
+        x_src = [x[b].rearrange("(p t) h w -> p t (h w)", t=PACK) for b in range(B)]
+        out_dst = [out[b].rearrange("(p t) h w -> p t (h w)", t=PACK) for b in range(B)]
+
+        chunks = {}
+        loads = []
+        for lo, width in ((0, 256), (256, 256), (512, 512)):
+            piece = keep.tile([P, PACK, width], BF16, name="xa0_%d" % lo)
+            chunks.setdefault(lo // NT, []).append((piece[:], lo % NT, width))
+            loads.append((piece[:], x_src[0][:, :, lo : lo + width]))
         for h in range(NH):
-            first = keep.tile([P, PACK, NT], BF16, name="xa0%d" % h)
-            xs[h] = first[:]
-        whole = {}
-        for b in range(1, B):
-            whole[b] = keep.tile([P, PACK, HW], BF16, name="xa%d" % b)
+            piece = keep.tile([P, PACK, NT], BF16, name="xa1_%d" % h)
+            chunks[NH + h] = [(piece[:], 0, NT)]
+            loads.append((piece[:], x_src[1][:, :, h * NT : (h + 1) * NT]))
+        for b in range(2, B):
+            whole = keep.tile([P, PACK, HW], BF16, name="xa%d" % b)
             for h in range(NH):
-                xs[NH * b + h] = whole[b][:, :, h * NT : (h + 1) * NT]
+                chunks[NH * b + h] = [(whole[:, :, h * NT : (h + 1) * NT], 0, NT)]
+            loads.append((whole[:], x_src[b]))
+
         res = [keep.tile([P, PACK, NT], F32, name="res%d" % u) for u in range(UNITS)]
         grouped = [keep.tile([P, NT, PACK], BF16, align_bytes=64, name="grouped%d" % u) for u in range(UNITS)]
         codes = [keep.tile([P, NT], U32, align_bytes=64, name="codes%d" % u) for u in range(UNITS)]
         planes = [keep.tile([P, NT], U8, align_bytes=64, name="planes%d" % u) for u in range(UNITS)]
-        x_src = [x[b].rearrange("(p t) h w -> p t (h w)", t=PACK) for b in range(B)]
-        out_dst = [out[b].rearrange("(p t) h w -> p t (h w)", t=PACK) for b in range(B)]
         acc = {}
 
         nc.vector.memset(s_raw[:].bitcast(I32), 0)
         nc.vector.memset(one[:], 1.0)
         nc.scalar.activation(out=warm[:], in_=one[:], func=ACT.Abs_reciprocal_sqrt)
 
-        nc.sync.dma_start(out=xs[0], in_=x_src[0][:, :, 0:NT])
+        nc.sync.dma_start(out=loads[0][0], in_=loads[0][1])
         nc.sync.dma_start(out=w_raw[:].bitcast(I32), in_=gamma_words[0].bitcast(I32))
         for q in range(4):
             nc.sync.dma_start(
                 out=s_raw[32 * q : 32 * q + 4, :].bitcast(I32),
                 in_=gamma_scales[0, 4 * q : 4 * q + 4, :].bitcast(I32),
             )
-        nc.sync.dma_start(out=xs[1], in_=x_src[0][:, :, NT:HW])
+        nc.sync.dma_start(out=loads[1][0], in_=loads[1][1])
+        nc.sync.dma_start(out=loads[2][0], in_=loads[2][1])
         nc.sync.dma_start(out=beta_bf[:], in_=beta.rearrange("(p t) -> p t", t=PACK))
-        for b in range(1, B):
-            nc.sync.dma_start(out=whole[b][:], in_=x_src[b])
+        for dst, src in loads[3:]:
+            nc.sync.dma_start(out=dst, in_=src)
 
-        def sq_v(u):
-            dst, src = regroup_views(grouped[u][:, 0:VW, :], xs[u][:, :, 0:VW], RUN)
-            nc.vector.tensor_tensor(out=dst, in0=src, in1=src, op=ALU.mult)
+        def sq_v(u, k=None):
+            for view, lo, width in chunks[u] if k is None else chunks[u][k : k + 1]:
+                vw = width * VNUM // VDEN
+                dst, src = regroup_views(grouped[u][:, lo : lo + vw, :], view[:, :, 0:vw], RUN)
+                nc.vector.tensor_tensor(out=dst, in0=src, in1=src, op=ALU.mult)
 
         def sq_s(u):
-            dst, src = regroup_views(grouped[u][:, VW:NT, :], xs[u][:, :, VW:NT], RUN)
-            nc.scalar.activation(out=dst, in_=src, func=ACT.Square)
+            for view, lo, width in chunks[u]:
+                vw = width * VNUM // VDEN
+                dst, src = regroup_views(grouped[u][:, lo + vw : lo + width, :], view[:, :, vw:width], RUN)
+                nc.scalar.activation(out=dst, in_=src, func=ACT.Square)
 
         def quant(u):
             nc.vector.quantize_mx(
@@ -119,43 +134,51 @@ def tile_gdn_kernel(tc, x, gamma_words, gamma_scales, beta, out):
             )
 
         def mul_store(u, t0, t1):
-            nc.vector.tensor_tensor(
-                out=res[u][:, t0:t1, :], in0=xs[u][:, t0:t1, :], in1=res[u][:, t0:t1, :], op=ALU.mult
-            )
+            for view, lo, width in chunks[u]:
+                nc.vector.tensor_tensor(
+                    out=res[u][:, t0:t1, lo : lo + width],
+                    in0=view[:, t0:t1, :],
+                    in1=res[u][:, t0:t1, lo : lo + width],
+                    op=ALU.mult,
+                )
             h = u % NH
             nc.sync.dma_start(out=out_dst[u // NH][:, t0:t1, h * NT : (h + 1) * NT], in_=res[u][:, t0:t1, :])
 
-        sq_v(0)
-        sq_s(0)
+        sq_v(0, 0)
         nc.vector.tensor_copy(
             out=w_words[:].rearrange("p (t q e) -> p q t e", t=PACK, e=2),
             in_=w_raw[:].rearrange("p (q t e) -> p q t e", t=PACK, e=2),
         )
+        sq_v(0, 1)
         nc.vector.tensor_copy(
             out=w_plane[:].rearrange("p (t q) -> p q t", t=PACK),
             in_=s_raw[:].rearrange("p (q t) -> p q t", t=PACK),
         )
-        quant(0)
-        for t in range(PACK):
-            mx(0, t)
+        for u in range(AHEAD):
+            sq_s(u)
+        for u in range(1, AHEAD):
+            sq_v(u)
+            quant(u - 1)
+        for u in range(AHEAD - 1):
+            for t in range(PACK):
+                mx(u, t)
 
-        for u in range(UNITS):
-            n = u + 1
-            more = n < UNITS
-            if more:
-                sq_v(n)
-                sq_s(n)
-            rs(u, 0)
-            if u > 0:
-                mul_store(u - 1, 2, 4)
-            if more:
-                quant(n)
-            rs(u, 1)
-            if more:
+        for i in range(UNITS):
+            if i + AHEAD < UNITS:
+                sq_v(i + AHEAD)
+            rs(i, 0)
+            rs(i, 1)
+            if i + AHEAD - 1 < UNITS:
+                quant(i + AHEAD - 1)
+            mul_store(i, 0, 2)
+            rs(i, 2)
+            rs(i, 3)
+            if i + AHEAD < UNITS:
+                sq_s(i + AHEAD)
+            if i + AHEAD - 1 < UNITS:
                 for t in range(PACK):
-                    mx(n, t)
-            mul_store(u, 0, 2)
-            rs(u, 2)
-            rs(u, 3)
+                    mx(i + AHEAD - 1, t)
+            if i + 1 < UNITS:
+                mul_store(i, 2, 4)
         mul_store(UNITS - 1, 2, 3)
         mul_store(UNITS - 1, 3, 4)

@@ -1,6 +1,7 @@
 from contextlib import ExitStack
 
 import concourse.mybir as mybir
+from concourse.masks import make_identity
 
 F32 = mybir.dt.float32
 BF16 = mybir.dt.bfloat16
@@ -20,10 +21,12 @@ PACK = 4
 NT = 512
 NH = HW // NT
 UNITS = B * NH
-VNUM = 3
-VDEN = 8
+VNUM = 7
+VDEN = 16
 RUN = 4
-AHEAD = 3
+AHEAD = 2
+ACC_BANKS = 5
+SHARED = (2, 4, 6, 7)
 
 FLOPS = 2 * C * C * B * HW
 
@@ -50,6 +53,7 @@ def tile_gdn_kernel(tc, x, gamma_words, gamma_scales, beta, out):
         beta_bf = const.tile([P, PACK], BF16)
         one = const.tile([P, 1], F32)
         warm = const.tile([P, 1], F32)
+        ident = const.tile([P, P], BF16)
 
         x_src = [x[b].rearrange("(p t) h w -> p t (h w)", t=PACK) for b in range(B)]
         out_dst = [out[b].rearrange("(p t) h w -> p t (h w)", t=PACK) for b in range(B)]
@@ -75,10 +79,12 @@ def tile_gdn_kernel(tc, x, gamma_words, gamma_scales, beta, out):
         codes = [keep.tile([P, NT], U32, align_bytes=64, name="codes%d" % u) for u in range(UNITS)]
         planes = [keep.tile([P, NT], U8, align_bytes=64, name="planes%d" % u) for u in range(UNITS)]
         acc = {}
+        xps = {}
 
         nc.vector.memset(s_raw[:].bitcast(I32), 0)
         nc.vector.memset(one[:], 1.0)
         nc.scalar.activation(out=warm[:], in_=one[:], func=ACT.Abs_reciprocal_sqrt)
+        make_identity(nc, ident[:])
 
         nc.sync.dma_start(out=loads[0][0], in_=loads[0][1])
         nc.sync.dma_start(out=w_raw[:].bitcast(I32), in_=gamma_words[0].bitcast(I32))
@@ -113,7 +119,7 @@ def tile_gdn_kernel(tc, x, gamma_words, gamma_scales, beta, out):
             )
 
         def mx(u, t):
-            acc[(u, t)] = psum.tile([P, NT], F32, name="bank%d" % (PACK * (u % 2) + t))
+            acc[(u, t)] = psum.tile([P, NT], F32, name="bank%d" % ((PACK * u + t) % ACC_BANKS))
             nc.tensor.matmul_mx(
                 out=acc[(u, t)][:],
                 lhsT=w_words[:, 2 * P * t : 2 * P * (t + 1)].bitcast(FP4X4),
@@ -144,6 +150,24 @@ def tile_gdn_kernel(tc, x, gamma_words, gamma_scales, beta, out):
             h = u % NH
             nc.sync.dma_start(out=out_dst[u // NH][:, t0:t1, h * NT : (h + 1) * NT], in_=res[u][:, t0:t1, :])
 
+        def store(u, t0, t1, src):
+            h = u % NH
+            nc.sync.dma_start(out=out_dst[u // NH][:, t0:t1, h * NT : (h + 1) * NT], in_=src)
+
+        def px(u, t):
+            xps[(u, t)] = psum.tile([P, NT], F32, name="xbank%d" % t)
+            nc.tensor.matmul(out=xps[(u, t)][:], lhsT=ident[:], rhs=chunks[u][0][0][:, t, :], start=True, stop=True)
+
+        def mul_p(u, t):
+            nc.vector.tensor_tensor(out=res[u][:, t, :], in0=xps[(u, t)][:], in1=res[u][:, t, :], op=ALU.mult)
+
+        def mul_g(u, t):
+            k = min(u + 1, UNITS - 1)
+            lo = (u + 1 - k) * NT
+            spare = grouped[k][:].rearrange("p w t -> p (w t)").bitcast(F32)[:, lo : lo + NT]
+            nc.gpsimd.tensor_tensor(out=spare, in0=chunks[u][0][0][:, t, :], in1=res[u][:, t, :], op=ALU.mult)
+            store(u, t, t + 1, spare.unsqueeze(1))
+
         sq_v(0, 0)
         nc.vector.tensor_copy(
             out=w_words[:].rearrange("p (t q e) -> p q t e", t=PACK, e=2),
@@ -156,21 +180,26 @@ def tile_gdn_kernel(tc, x, gamma_words, gamma_scales, beta, out):
         )
         for u in range(AHEAD):
             sq_s(u)
+        quant(0)
         for u in range(1, AHEAD):
             sq_v(u)
-            quant(u - 1)
         for u in range(AHEAD - 1):
             for t in range(PACK):
                 mx(u, t)
 
         for i in range(UNITS):
+            shared = i in SHARED
             if i + AHEAD < UNITS:
                 sq_v(i + AHEAD)
             rs(i, 0)
             rs(i, 1)
             if i + AHEAD - 1 < UNITS:
                 quant(i + AHEAD - 1)
-            mul_store(i, 0, 2)
+            if shared:
+                mul_g(i, 0)
+                mul_p(i, 1)
+            else:
+                mul_store(i, 0, 2)
             rs(i, 2)
             rs(i, 3)
             if i + AHEAD < UNITS:
@@ -178,7 +207,17 @@ def tile_gdn_kernel(tc, x, gamma_words, gamma_scales, beta, out):
             if i + AHEAD - 1 < UNITS:
                 for t in range(PACK):
                     mx(i + AHEAD - 1, t)
-            if i + 1 < UNITS:
+            if shared:
+                mul_p(i, 2)
+                if i + 1 == UNITS:
+                    store(i, 1, 3, res[i][:, 1:3, :])
+                mul_p(i, 3)
+                if i + 1 == UNITS:
+                    store(i, 3, 4, res[i][:, 3:4, :])
+                else:
+                    store(i, 1, 4, res[i][:, 1:4, :])
+            else:
                 mul_store(i, 2, 4)
-        mul_store(UNITS - 1, 2, 3)
-        mul_store(UNITS - 1, 3, 4)
+            if i + 1 in SHARED:
+                for t in range(1, PACK):
+                    px(i + 1, t)

@@ -23,7 +23,7 @@ NH = HW // NT
 UNITS = B * NH
 VNUM = 7
 VDEN = 16
-RUN = 4
+RUN = 2
 AHEAD = 2
 ACC_BANKS = 5
 SHARED = (2, 4, 6, 7)

@@ -21,8 +21,8 @@ PACK = 4
 NT = 512
 NH = HW // NT
 UNITS = B * NH
-VNUM = 7
-VDEN = 16
+VNUM = 13
+VDEN = 32
 RUN = 2
 AHEAD = 2
 ACC_BANKS = 5

@@ -21,8 +21,8 @@ PACK = 4
 NT = 512
 NH = HW // NT
 UNITS = B * NH
-VNUM = 13
-VDEN = 32
+VNUM = 53
+VDEN = 128
 RUN = 2
 AHEAD = 2
 ACC_BANKS = 5

@@ -21,12 +21,12 @@ PACK = 4
 NT = 512
 NH = HW // NT
 UNITS = B * NH
-VNUM = 53
-VDEN = 128
+VNUM = 7
+VDEN = 16
 RUN = 2
 AHEAD = 2
 ACC_BANKS = 5
-SHARED = (2, 4, 6, 7)
+SHARED = (2, 4, 5, 6)
 
 FLOPS = 2 * C * C * B * HW
 
@@ -198,6 +198,9 @@ def tile_gdn_kernel(tc, x, gamma_words, gamma_scales, beta, out):
             if shared:
                 mul_g(i, 0)
                 mul_p(i, 1)
+            elif i + 1 == UNITS:
+                mul_store(i, 0, 1)
+                mul_store(i, 1, 2)
             else:
                 mul_store(i, 0, 2)
             rs(i, 2)
@@ -209,13 +212,11 @@ def tile_gdn_kernel(tc, x, gamma_words, gamma_scales, beta, out):
                     mx(i + AHEAD - 1, t)
             if shared:
                 mul_p(i, 2)
-                if i + 1 == UNITS:
-                    store(i, 1, 3, res[i][:, 1:3, :])
                 mul_p(i, 3)
-                if i + 1 == UNITS:
-                    store(i, 3, 4, res[i][:, 3:4, :])
-                else:
-                    store(i, 1, 4, res[i][:, 1:4, :])
+                store(i, 1, 4, res[i][:, 1:4, :])
+            elif i + 1 == UNITS:
+                mul_store(i, 2, 3)
+                mul_store(i, 3, 4)
             else:
                 mul_store(i, 2, 4)
             if i + 1 in SHARED:

from contextlib import ExitStack

import concourse.mybir as mybir
from concourse.masks import make_identity

F32 = mybir.dt.float32
BF16 = mybir.dt.bfloat16
I32 = mybir.dt.int32
U32 = mybir.dt.uint32
U8 = mybir.dt.uint8
FP8X4 = mybir.dt.float8_e4m3fn_x4
FP4X4 = mybir.dt.float4_e2m1fn_x4
ACT = mybir.ActivationFunctionType
ALU = mybir.AluOpType

P = 128
B = 4
C = 512
HW = 1024
PACK = 4
NT = 512
NH = HW // NT
UNITS = B * NH
VNUM = 7
VDEN = 16
RUN = 2
AHEAD = 2
ACC_BANKS = 5
SHARED = (2, 4, 5, 6)

FLOPS = 2 * C * C * B * HW


def regroup_views(dst, src, run):
    return (
        dst.rearrange("p (c i) t -> p c t i", i=run),
        src.rearrange("p t (c i) -> p c t i", i=run),
    )


def tile_gdn_kernel(tc, x, gamma_words, gamma_scales, beta, out):
    nc = tc.nc
    with ExitStack() as ctx:
        const = ctx.enter_context(tc.tile_pool(name="const", bufs=1))
        keep = ctx.enter_context(tc.tile_pool(name="keep", bufs=1))
        psum = ctx.enter_context(tc.psum_pool(name="psum", bufs=1))
        ctx.enter_context(tc.manual_schedule())

        w_raw = const.tile([P, 2 * C], U8, align_bytes=64)
        w_words = const.tile([P, 2 * C], U8, align_bytes=64)
        s_raw = const.tile([P, C], U8, align_bytes=64)
        w_plane = const.tile([P, C], U8, align_bytes=64)
        beta_bf = const.tile([P, PACK], BF16)
        one = const.tile([P, 1], F32)
        warm = const.tile([P, 1], F32)
        ident = const.tile([P, P], BF16)

        x_src = [x[b].rearrange("(p t) h w -> p t (h w)", t=PACK) for b in range(B)]
        out_dst = [out[b].rearrange("(p t) h w -> p t (h w)", t=PACK) for b in range(B)]

        chunks = {}
        loads = []
        for lo, width in ((0, 256), (256, 256), (512, 512)):
            piece = keep.tile([P, PACK, width], BF16, name="xa0_%d" % lo)
            chunks.setdefault(lo // NT, []).append((piece[:], lo % NT, width))
            loads.append((piece[:], x_src[0][:, :, lo : lo + width]))
        for h in range(NH):
            piece = keep.tile([P, PACK, NT], BF16, name="xa1_%d" % h)
            chunks[NH + h] = [(piece[:], 0, NT)]
            loads.append((piece[:], x_src[1][:, :, h * NT : (h + 1) * NT]))
        for b in range(2, B):
            whole = keep.tile([P, PACK, HW], BF16, name="xa%d" % b)
            for h in range(NH):
                chunks[NH * b + h] = [(whole[:, :, h * NT : (h + 1) * NT], 0, NT)]
            loads.append((whole[:], x_src[b]))

        res = [keep.tile([P, PACK, NT], F32, name="res%d" % u) for u in range(UNITS)]
        grouped = [keep.tile([P, NT, PACK], BF16, align_bytes=64, name="grouped%d" % u) for u in range(UNITS)]
        codes = [keep.tile([P, NT], U32, align_bytes=64, name="codes%d" % u) for u in range(UNITS)]
        planes = [keep.tile([P, NT], U8, align_bytes=64, name="planes%d" % u) for u in range(UNITS)]
        acc = {}
        xps = {}

        nc.vector.memset(s_raw[:].bitcast(I32), 0)
        nc.vector.memset(one[:], 1.0)
        nc.scalar.activation(out=warm[:], in_=one[:], func=ACT.Abs_reciprocal_sqrt)
        make_identity(nc, ident[:])

        nc.sync.dma_start(out=loads[0][0], in_=loads[0][1])
        nc.sync.dma_start(out=w_raw[:].bitcast(I32), in_=gamma_words[0].bitcast(I32))
        for q in range(4):
            nc.sync.dma_start(
                out=s_raw[32 * q : 32 * q + 4, :].bitcast(I32),
                in_=gamma_scales[0, 4 * q : 4 * q + 4, :].bitcast(I32),
            )
        nc.sync.dma_start(out=loads[1][0], in_=loads[1][1])
        nc.sync.dma_start(out=loads[2][0], in_=loads[2][1])
        nc.sync.dma_start(out=beta_bf[:], in_=beta.rearrange("(p t) -> p t", t=PACK))
        for dst, src in loads[3:]:
            nc.sync.dma_start(out=dst, in_=src)

        def sq_v(u, k=None):
            for view, lo, width in chunks[u] if k is None else chunks[u][k : k + 1]:
                vw = width * VNUM // VDEN
                dst, src = regroup_views(grouped[u][:, lo : lo + vw, :], view[:, :, 0:vw], RUN)
                nc.vector.tensor_tensor(out=dst, in0=src, in1=src, op=ALU.mult)

        def sq_s(u):
            for view, lo, width in chunks[u]:
                vw = width * VNUM // VDEN
                dst, src = regroup_views(grouped[u][:, lo + vw : lo + width, :], view[:, :, vw:width], RUN)
                nc.scalar.activation(out=dst, in_=src, func=ACT.Square)

        def quant(u):
            nc.vector.quantize_mx(
                out=codes[u][:].bitcast(FP8X4),
                scales=planes[u][:],
                in_=grouped[u][:].rearrange("p w t -> p (w t)"),
            )

        def mx(u, t):
            acc[(u, t)] = psum.tile([P, NT], F32, name="bank%d" % ((PACK * u + t) % ACC_BANKS))
            nc.tensor.matmul_mx(
                out=acc[(u, t)][:],
                lhsT=w_words[:, 2 * P * t : 2 * P * (t + 1)].bitcast(FP4X4),
                lhsT_scale=w_plane[:, P * t : P * (t + 1)],
                rhs=codes[u][:].bitcast(FP8X4),
                rhs_scale=planes[u][:],
                start=True,
                stop=True,
            )

        def rs(u, t):
            nc.scalar.activation(
                out=res[u][:, t, :],
                in_=acc[(u, t)][:],
                func=ACT.Abs_reciprocal_sqrt,
                bias=beta_bf[:, t : t + 1],
                scale=1.0,
            )

        def mul_store(u, t0, t1):
            for view, lo, width in chunks[u]:
                nc.vector.tensor_tensor(
                    out=res[u][:, t0:t1, lo : lo + width],
                    in0=view[:, t0:t1, :],
                    in1=res[u][:, t0:t1, lo : lo + width],
                    op=ALU.mult,
                )
            h = u % NH
            nc.sync.dma_start(out=out_dst[u // NH][:, t0:t1, h * NT : (h + 1) * NT], in_=res[u][:, t0:t1, :])

        def store(u, t0, t1, src):
            h = u % NH
            nc.sync.dma_start(out=out_dst[u // NH][:, t0:t1, h * NT : (h + 1) * NT], in_=src)

        def px(u, t):
            xps[(u, t)] = psum.tile([P, NT], F32, name="xbank%d" % t)
            nc.tensor.matmul(out=xps[(u, t)][:], lhsT=ident[:], rhs=chunks[u][0][0][:, t, :], start=True, stop=True)

        def mul_p(u, t):
            nc.vector.tensor_tensor(out=res[u][:, t, :], in0=xps[(u, t)][:], in1=res[u][:, t, :], op=ALU.mult)

        def mul_g(u, t):
            k = min(u + 1, UNITS - 1)
            lo = (u + 1 - k) * NT
            spare = grouped[k][:].rearrange("p w t -> p (w t)").bitcast(F32)[:, lo : lo + NT]
            nc.gpsimd.tensor_tensor(out=spare, in0=chunks[u][0][0][:, t, :], in1=res[u][:, t, :], op=ALU.mult)
            store(u, t, t + 1, spare.unsqueeze(1))

        sq_v(0, 0)
        nc.vector.tensor_copy(
            out=w_words[:].rearrange("p (t q e) -> p q t e", t=PACK, e=2),
            in_=w_raw[:].rearrange("p (q t e) -> p q t e", t=PACK, e=2),
        )
        sq_v(0, 1)
        nc.vector.tensor_copy(
            out=w_plane[:].rearrange("p (t q) -> p q t", t=PACK),
            in_=s_raw[:].rearrange("p (q t) -> p q t", t=PACK),
        )
        for u in range(AHEAD):
            sq_s(u)
        quant(0)
        for u in range(1, AHEAD):
            sq_v(u)
        for u in range(AHEAD - 1):
            for t in range(PACK):
                mx(u, t)

        for i in range(UNITS):
            shared = i in SHARED
            if i + AHEAD < UNITS:
                sq_v(i + AHEAD)
            rs(i, 0)
            rs(i, 1)
            if i + AHEAD - 1 < UNITS:
                quant(i + AHEAD - 1)
            if shared:
                mul_g(i, 0)
                mul_p(i, 1)
            elif i + 1 == UNITS:
                mul_store(i, 0, 1)
                mul_store(i, 1, 2)
            else:
                mul_store(i, 0, 2)
            rs(i, 2)
            rs(i, 3)
            if i + AHEAD < UNITS:
                sq_s(i + AHEAD)
            if i + AHEAD - 1 < UNITS:
                for t in range(PACK):
                    mx(i + AHEAD - 1, t)
            if shared:
                mul_p(i, 2)
                mul_p(i, 3)
                store(i, 1, 4, res[i][:, 1:4, :])
            elif i + 1 == UNITS:
                mul_store(i, 2, 3)
                mul_store(i, 3, 4)
            else:
                mul_store(i, 2, 4)
            if i + 1 in SHARED:
                for t in range(1, PACK):
                    px(i + 1, t)
